import numpy as np
import ml_dtypes


def mxq(x, axis, fmt="e4m3"):
    dtype, down = {"e4m3": (ml_dtypes.float8_e4m3fn, 7), "e5m2": (ml_dtypes.float8_e5m2, 14)}[fmt]
    v = np.moveaxis(np.asarray(x, np.float32).astype(ml_dtypes.bfloat16).astype(np.float64), axis, -1)
    blocks = v.reshape(v.shape[:-1] + (-1, 32))
    amax = np.abs(blocks).max(-1, keepdims=True)
    byte = np.maximum(np.where(amax > 0, np.frexp(amax)[1] - 1 + 127, 0) - down, 1)
    scale = np.exp2(byte - 127.0)
    codes = (blocks / scale).astype(np.float32).astype(dtype).astype(np.float64)
    return np.moveaxis((codes * scale).reshape(v.shape), -1, axis)


WIDE = False


def mx_kscale(k):
    if not WIDE:
        return np.ones(k)
    levels = np.array([10, -10, 5, -5, 0])
    a = np.random.permutation(np.resize(levels, k // 512 * 4)).reshape(k // 512, 4)
    idx = np.arange(k)
    return np.exp2(a[idx // 512, idx % 128 // 32])


BF16 = ml_dtypes.bfloat16


def bf(x):
    return np.asarray(x, np.float32).astype(BF16)


def f64(x):
    return np.asarray(x).astype(np.float64)


B, T, D, F = 2, 512, 512, 512
BINS = np.array([-1.5, -1.0, -0.5, 0.0, 0.5, 1.0, 1.5])
NB = BINS.shape[0] + 1
INDEX = 0


def setup_inputs():
    s = mx_kscale(D)
    s = s / s[INDEX]
    return {"x": bf(np.random.standard_normal((B, T, D)) * s),
            "W": bf(np.random.standard_normal((NB, D, F)) * 0.5 / np.sqrt(D) / s[None, :, None])}


def reference(x, W):
    x, W = f64(x), f64(W)
    y = x[..., INDEX]
    mem = np.sum(np.where(y[..., None] > BINS, 1.0, 0.0), axis=-1)
    xf = x.reshape(B * T, D)
    memf = mem.reshape(B * T)
    xq = mxq(xf, 1, "e4m3")
    Wq = mxq(W, 1, "e4m3")
    out = np.zeros((B * T, F))
    for k in range(NB):
        sel = np.where(memf == k, 1.0, 0.0)[:, None]
        out = out + sel * (xq @ Wq[k])
    return out.reshape(B, T, F)

@@ -1,0 +1,259 @@
+from contextlib import ExitStack
+
+import concourse.mybir as mybir
+
+FLOPS = 2 * 1024 * 512 * 512 * 8
+
+F32 = mybir.dt.float32
+BF16 = mybir.dt.bfloat16
+U32 = mybir.dt.uint32
+U8 = mybir.dt.uint8
+FP8X4 = mybir.dt.float8_e4m3fn_x4
+ALU = mybir.AluOpType
+ACT = mybir.ActivationFunctionType
+AX = mybir.AxisListType
+
+P = 128
+NT = 8
+D = 512
+F = 512
+NE = 8
+L = 4
+BOUNDS = (-1.5, -1.0, -0.5, 0.0, 0.5, 1.0, 1.5)
+MID = 3
+FV = [352,352,352,352,352,352,352,352]
+X_GROUPS = ((0, 1), (2, 3), (4, 5, 6, 7))
+T_BANKS = ((0, 1), (2, 3), (4, 5), (6, 7), (4, 5), (6, 7), (4, 5), (6, 7))
+W_AFTER = {1: (1,), 3: (2,), 5: (3,)}
+PINNED = True
+
+
+def tile_dispatchbyvariable_pa_kernel(tc, x, W, out):
+    nc = tc.nc
+    x_v = x.flatten_outer_dims().rearrange("(p j) d -> p j d", j=NT)
+    o_v = out.flatten_outer_dims().rearrange("(p j) f -> p j f", j=NT)
+    nb = len(BOUNDS)
+    where = {}
+    for g, tiles in enumerate(X_GROUPS):
+        for i, j in enumerate(tiles):
+            where[j] = (g, i)
+
+    with ExitStack() as ctx:
+        if PINNED:
+            ctx.enter_context(tc.manual_schedule())
+        keep = ctx.enter_context(tc.tile_pool(name="keep", bufs=1))
+        psum = ctx.enter_context(tc.psum_pool(name="psum", bufs=1))
+
+        xh = [keep.tile([P, len(t), D], BF16, name="xh%d" % g) for g, t in enumerate(X_GROUPS)]
+        raw = [keep.tile([P, 4, F], BF16, name="raw%d" % k) for k in range(NE)]
+
+        def load_x(g):
+            t = X_GROUPS[g]
+            nc.sync.dma_start(out=xh[g][:], in_=x_v[:, t[0] : t[0] + len(t), :])
+
+        def load_w(k):
+            nc.sync.dma_start(
+                out=raw[k][:].rearrange("p (u e) f -> p u (e f)", u=2),
+                in_=W[k].rearrange("(u p e) f -> p u (e f)", u=2, e=2),
+            )
+
+        load_x(0)
+        load_w(0)
+        load_x(1)
+        load_x(2)
+        for k in range(1, NE):
+            load_w(k)
+
+        col_i = keep.tile([P, L * P], F32, name="col_i")
+        nc.gpsimd.iota(
+            col_i[:], pattern=[[1, L * P]], base=0, channel_multiplier=-1,
+            allow_small_or_imprecise_dtypes=True,
+        )
+        bins = keep.tile([P, nb], F32, name="bins")
+        for i, b in enumerate(BOUNDS):
+            nc.vector.memset(bins[:, i : i + 1], b)
+        warm = keep.tile([P, 1], F32, name="warm")
+        nc.scalar.activation(out=warm[:], in_=bins[:, 0:1], func=ACT.Copy)
+        colv = keep.tile([P, L * P], F32, name="colv")
+        nc.vector.tensor_scalar(
+            out=colv[:], in0=col_i[:], scalar1=1.0 / P, scalar2=None, op0=ALU.mult
+        )
+
+        gt = [keep.tile([P, len(t), nb], F32, name="gt%d" % g) for g, t in enumerate(X_GROUPS)]
+        cnt = [keep.tile([P, len(t)], F32, name="cnt%d" % g) for g, t in enumerate(X_GROUPS)]
+        lo = [keep.tile([P, len(t)], F32, name="lo%d" % g) for g, t in enumerate(X_GROUPS)]
+        hi0 = [keep.tile([P, len(t)], F32, name="hi0_%d" % g) for g, t in enumerate(X_GROUPS)]
+
+        def bucket(g):
+            shape = [P, len(X_GROUPS[g]), nb]
+            nc.vector.tensor_tensor(
+                out=gt[g][:],
+                in0=xh[g][:, :, 0:1].to_broadcast(shape),
+                in1=bins[:].unsqueeze(1).to_broadcast(shape),
+                op=ALU.is_gt,
+            )
+            nc.vector.tensor_reduce(out=cnt[g][:], in_=gt[g][:], axis=AX.X, op=ALU.add)
+            nc.vector.scalar_tensor_tensor(
+                out=lo[g][:], in0=gt[g][:, :, MID], scalar=-float(L), in1=cnt[g][:],
+                op0=ALU.mult, op1=ALU.add,
+            )
+            nc.vector.tensor_scalar(
+                out=hi0[g][:], in0=gt[g][:, :, MID], scalar1=-1.0, scalar2=1.0,
+                op0=ALU.mult, op1=ALU.add,
+            )
+
+        sel = [keep.tile([P, L * P], F32, name="sel%d" % j) for j in range(NT)]
+        xg = [keep.tile([P, L * P * 4], BF16, name="xg%d" % j, align_bytes=64) for j in range(NT)]
+        xq = [keep.tile([P, L * P], U32, name="xq%d" % j, align_bytes=64) for j in range(NT)]
+        xs = [keep.tile([P, L * P], U8, name="xs%d" % j, align_bytes=64) for j in range(NT)]
+        pts = {}
+
+        def sel_and_transpose(j):
+            g, i = where[j]
+            if i == 0:
+                bucket(g)
+            nc.vector.tensor_scalar(
+                out=sel[j][:], in0=colv[:], scalar1=lo[g][:, i : i + 1],
+                scalar2=None, op0=ALU.is_equal,
+            )
+            words = xh[g][:].rearrange("p j d -> p (j d)").bitcast(F32)
+            for half in range(2):
+                pt = psum.tile(
+                    [P, 2, 2, P], F32, tag="bank%d" % T_BANKS[j][half], name="pt%d_%d" % (j, half)
+                )
+                pts[(j, half)] = pt
+                for u in range(2):
+                    c0 = i * (D // 2) + u * P
+                    for li in range(2):
+                        c = 2 * half + li
+                        nc.tensor.transpose(
+                            out=pt[:, li, u, :],
+                            in_=words[:, c0 : c0 + P],
+                            identity=sel[j][:, c * P : (c + 1) * P],
+                        )
+
+        def copy_out(j):
+            dst = xg[j][:].bitcast(F32).rearrange("p (l t u) -> p l t u", l=L, u=2)
+            for half in range(2):
+                nc.scalar.copy(
+                    out=dst[:, 2 * half : 2 * half + 2, :, :],
+                    in_=pts[(j, half)][:].rearrange("p l u t -> p l t u"),
+                )
+
+        def quant_x(j):
+            nc.vector.quantize_mx(out=xq[j][:].bitcast(FP8X4), scales=xs[j][:], in_=xg[j][:])
+
+        wg = [keep.tile([P, F, 4], BF16, name="wg%d" % k, align_bytes=64) for k in range(NE)]
+        wq = [keep.tile([P, F], U32, name="wq%d" % k, align_bytes=64) for k in range(NE)]
+        ws = [keep.tile([P, F], U8, name="ws%d" % k, align_bytes=64) for k in range(NE)]
+
+        def regroup(k):
+            fv = FV[k]
+            if fv > 0:
+                nc.vector.tensor_copy(
+                    out=wg[k][:, 0:fv, :].rearrange("p (c i) t -> p c t i", i=4),
+                    in_=raw[k][:, :, 0:fv].rearrange("p t (c i) -> p c t i", i=4),
+                )
+            if fv < F:
+                nc.scalar.copy(
+                    out=wg[k][:, fv:F, :].rearrange("p (c i) t -> p c t i", i=4),
+                    in_=raw[k][:, :, fv:F].rearrange("p t (c i) -> p c t i", i=4),
+                )
+
+        def quant_w(k):
+            nc.vector.quantize_mx(
+                out=wq[k][:].bitcast(FP8X4), scales=ws[k][:],
+                in_=wg[k][:].rearrange("p f t -> p (f t)"),
+            )
+
+        acc = {}
+
+        def mx(j, k):
+            h, c = k // L, k % L
+            if c == 0:
+                acc[(j, h)] = psum.tile([P, F], F32, tag="bank%d" % j, name="acc%d_%d" % (j, h))
+            nc.tensor.matmul_mx(
+                out=acc[(j, h)][:],
+                lhsT=xq[j][:, c * P : (c + 1) * P].bitcast(FP8X4),
+                lhsT_scale=xs[j][:, c * P : (c + 1) * P],
+                rhs=wq[k][:].bitcast(FP8X4),
+                rhs_scale=ws[k][:],
+                start=(c == 0),
+                stop=(c == L - 1),
+            )
+
+        part = [keep.tile([P, F], F32, name="part%d" % j) for j in range(NT)]
+        res = [keep.tile([P, F], F32, name="res%d" % j) for j in range(NT)]
+
+        def first_half(j):
+            g, i = where[j]
+            nc.scalar.activation(
+                out=part[j][:], in_=acc[(j, 0)][:], func=ACT.Copy, scale=hi0[g][:, i : i + 1]
+            )
+
+        def second_half(j):
+            g, i = where[j]
+            nc.vector.scalar_tensor_tensor(
+                out=res[j][:], in0=acc[(j, 1)][:], scalar=gt[g][:, i, MID : MID + 1],
+                in1=part[j][:], op0=ALU.mult, op1=ALU.add,
+            )
+            nc.sync.dma_start(out=o_v[:, j, :], in_=res[j][:])
+
+        sel_and_transpose(0)
+        sel_and_transpose(1)
+        regroup(0)
+        sel_and_transpose(2)
+        sel_and_transpose(3)
+        pending = [0]
+        ready_x = []
+        ready_w = []
+        late = []
+        for j in range(NT):
+            copy_out(j)
+            if 2 <= j < NT - 2:
+                sel_and_transpose(j + 2)
+            for k in pending:
+                quant_w(k)
+                ready_w.append(k)
+                for t in ready_x:
+                    if t < 4:
+                        mx(t, k)
+                    else:
+                        late.append((k, t))
+            pending = []
+            for k in W_AFTER.get(j, ()):
+                regroup(k)
+                pending.append(k)
+            quant_x(j)
+            ready_x.append(j)
+            for k in ready_w:
+                if j < 4:
+                    mx(j, k)
+                else:
+                    late.append((k, j))
+        for k in pending:
+            quant_w(k)
+            for t in range(NT):
+                if t < 4:
+                    mx(t, k)
+                else:
+                    late.append((k, t))
+        for k, t in sorted(late):
+            mx(t, k)
+        regroup(4)
+        regroup(5)
+        quant_w(4)
+        quant_w(5)
+        regroup(6)
+        regroup(7)
+        for j in range(NT):
+            first_half(j)
+        quant_w(6)
+        quant_w(7)
+        for k in (4, 5):
+            for j in range(NT):
+                mx(j, k)
+        for j in range(NT):
+            mx(j, 6)
+            mx(j, 7)
+            second_half(j)

@@ -21,7 +21,7 @@ NE = 8
 L = 4
 BOUNDS = (-1.5, -1.0, -0.5, 0.0, 0.5, 1.0, 1.5)
 MID = 3
-FV = [352,352,352,352,352,352,352,352]
+FV = [320,320,320,320,320,320,320,320]
 X_GROUPS = ((0, 1), (2, 3), (4, 5, 6, 7))
 T_BANKS = ((0, 1), (2, 3), (4, 5), (6, 7), (4, 5), (6, 7), (4, 5), (6, 7))
 W_AFTER = {1: (1,), 3: (2,), 5: (3,)}
@@ -97,9 +97,10 @@ def tile_dispatchbyvariable_pa_kernel(tc, x, W, out):
                 out=lo[g][:], in0=gt[g][:, :, MID], scalar=-float(L), in1=cnt[g][:],
                 op0=ALU.mult, op1=ALU.add,
             )
-            nc.vector.tensor_scalar(
-                out=hi0[g][:], in0=gt[g][:, :, MID], scalar1=-1.0, scalar2=1.0,
-                op0=ALU.mult, op1=ALU.add,
+
+        def make_hi0(g):
+            nc.scalar.activation(
+                out=hi0[g][:], in_=gt[g][:, :, MID], func=ACT.Copy, scale=-1.0, bias=1.0
             )
 
         sel = [keep.tile([P, L * P], F32, name="sel%d" % j) for j in range(NT)]
@@ -207,7 +208,6 @@ def tile_dispatchbyvariable_pa_kernel(tc, x, W, out):
         pending = [0]
         ready_x = []
         ready_w = []
-        late = []
         for j in range(NT):
             copy_out(j)
             if 2 <= j < NT - 2:
@@ -218,42 +218,41 @@ def tile_dispatchbyvariable_pa_kernel(tc, x, W, out):
                 for t in ready_x:
                     if t < 4:
                         mx(t, k)
-                    else:
-                        late.append((k, t))
             pending = []
             for k in W_AFTER.get(j, ()):
                 regroup(k)
                 pending.append(k)
             quant_x(j)
             ready_x.append(j)
-            for k in ready_w:
-                if j < 4:
+            if j < 4:
+                for k in ready_w:
                     mx(j, k)
-                else:
-                    late.append((k, j))
-        for k in pending:
-            quant_w(k)
-            for t in range(NT):
-                if t < 4:
-                    mx(t, k)
-                else:
-                    late.append((k, t))
-        for k, t in sorted(late):
-            mx(t, k)
         regroup(4)
         regroup(5)
+        for g in range(len(X_GROUPS)):
+            make_hi0(g)
+        for j in range(4):
+            first_half(j)
         quant_w(4)
         quant_w(5)
         regroup(6)
         regroup(7)
-        for j in range(NT):
-            first_half(j)
-        quant_w(6)
-        quant_w(7)
-        for k in (4, 5):
-            for j in range(NT):
+        for j in range(4, NT):
+            for k in range(L):
                 mx(j, k)
-        for j in range(NT):
+            first_half(j)
+            if j == 4:
+                quant_w(6)
+            if j == 5:
+                quant_w(7)
+        for k in (4, 5):
+            for j in range(4):
+                mx(j, k)
+        for j in range(4):
             mx(j, 6)
             mx(j, 7)
+            second_half(j)
+        for j in range(4, NT):
+            for k in range(L, NE):
+                mx(j, k)
             second_half(j)

@@ -200,6 +200,27 @@ def tile_dispatchbyvariable_pa_kernel(tc, x, W, out):
             )
             nc.sync.dma_start(out=o_v[:, j, :], in_=res[j][:])
 
+        def last_tile_half(half, bank):
+            j = NT - 1
+            g, i = where[j]
+            cols = slice(half * (F // 2), (half + 1) * (F // 2))
+            ps = psum.tile([P, F // 2], F32, tag="bank%d" % bank, name="last%d" % half)
+            for c in range(L):
+                nc.tensor.matmul_mx(
+                    out=ps[:],
+                    lhsT=xq[j][:, c * P : (c + 1) * P].bitcast(FP8X4),
+                    lhsT_scale=xs[j][:, c * P : (c + 1) * P],
+                    rhs=wq[L + c][:, cols].bitcast(FP8X4),
+                    rhs_scale=ws[L + c][:, cols],
+                    start=(c == 0),
+                    stop=(c == L - 1),
+                )
+            nc.vector.scalar_tensor_tensor(
+                out=res[j][:, cols], in0=ps[:], scalar=gt[g][:, i, MID : MID + 1],
+                in1=part[j][:, cols], op0=ALU.mult, op1=ALU.add,
+            )
+            nc.sync.dma_start(out=o_v[:, j, cols], in_=res[j][:, cols])
+
         sel_and_transpose(0)
         sel_and_transpose(1)
         regroup(0)
@@ -252,7 +273,9 @@ def tile_dispatchbyvariable_pa_kernel(tc, x, W, out):
             mx(j, 6)
             mx(j, 7)
             second_half(j)
-        for j in range(4, NT):
+        for j in range(4, NT - 1):
             for k in range(L, NE):
                 mx(j, k)
             second_half(j)
+        for half, bank in enumerate((NT - 1, 0)):
+            last_tile_half(half, bank)

@@ -69,38 +69,41 @@ def tile_dispatchbyvariable_pa_kernel(tc, x, W, out):
             col_i[:], pattern=[[1, L * P]], base=0, channel_multiplier=-1,
             allow_small_or_imprecise_dtypes=True,
         )
-        bins = keep.tile([P, nb], F32, name="bins")
-        for i, b in enumerate(BOUNDS):
+        bins = keep.tile([P, nb - 1], F32, name="bins")
+        for i, b in enumerate(BOUNDS[:MID] + BOUNDS[MID + 1 :]):
             nc.vector.memset(bins[:, i : i + 1], b)
         warm = keep.tile([P, 1], F32, name="warm")
         nc.scalar.activation(out=warm[:], in_=bins[:, 0:1], func=ACT.Copy)
         colv = keep.tile([P, L * P], F32, name="colv")
         nc.vector.tensor_scalar(
-            out=colv[:], in0=col_i[:], scalar1=1.0 / P, scalar2=None, op0=ALU.mult
+            out=colv[:], in0=col_i[:], scalar1=1.0 / P, scalar2=float(MID), op0=ALU.mult, op1=ALU.add
         )
 
-        gt = [keep.tile([P, len(t), nb], F32, name="gt%d" % g) for g, t in enumerate(X_GROUPS)]
-        cnt = [keep.tile([P, len(t)], F32, name="cnt%d" % g) for g, t in enumerate(X_GROUPS)]
+        ncmp = nb - 1 + MID
+        cmp = [keep.tile([P, len(t), ncmp], F32, name="cmp%d" % g) for g, t in enumerate(X_GROUPS)]
         lo = [keep.tile([P, len(t)], F32, name="lo%d" % g) for g, t in enumerate(X_GROUPS)]
-        hi0 = [keep.tile([P, len(t)], F32, name="hi0_%d" % g) for g, t in enumerate(X_GROUPS)]
+        hi1 = [keep.tile([P, len(t)], F32, name="hi1_%d" % g) for g, t in enumerate(X_GROUPS)]
 
-        def bucket(g):
-            shape = [P, len(X_GROUPS[g]), nb]
+        def bucket_cmp(g):
+            n = len(X_GROUPS[g])
             nc.vector.tensor_tensor(
-                out=gt[g][:],
-                in0=xh[g][:, :, 0:1].to_broadcast(shape),
-                in1=bins[:].unsqueeze(1).to_broadcast(shape),
+                out=cmp[g][:, :, 0 : nb - 1],
+                in0=xh[g][:, :, 0:1].to_broadcast([P, n, nb - 1]),
+                in1=bins[:].unsqueeze(1).to_broadcast([P, n, nb - 1]),
                 op=ALU.is_gt,
             )
-            nc.vector.tensor_reduce(out=cnt[g][:], in_=gt[g][:], axis=AX.X, op=ALU.add)
-            nc.vector.scalar_tensor_tensor(
-                out=lo[g][:], in0=gt[g][:, :, MID], scalar=-float(L), in1=cnt[g][:],
-                op0=ALU.mult, op1=ALU.add,
+            nc.vector.tensor_scalar(
+                out=cmp[g][:, :, nb - 1 : ncmp],
+                in0=xh[g][:, :, 0:1].to_broadcast([P, n, MID]),
+                scalar1=BOUNDS[MID], scalar2=0.0, op0=ALU.is_gt, op1=ALU.is_equal,
             )
 
-        def make_hi0(g):
-            nc.scalar.activation(
-                out=hi0[g][:], in_=gt[g][:, :, MID], func=ACT.Copy, scale=-1.0, bias=1.0
+        def bucket_sum(g):
+            nc.vector.tensor_reduce(out=lo[g][:], in_=cmp[g][:], axis=AX.X, op=ALU.add)
+
+        def make_hi1(g):
+            nc.vector.tensor_scalar(
+                out=hi1[g][:], in0=xh[g][:, :, 0], scalar1=BOUNDS[MID], scalar2=None, op0=ALU.is_gt
             )
 
         sel = [keep.tile([P, L * P], F32, name="sel%d" % j) for j in range(NT)]
@@ -111,8 +114,6 @@ def tile_dispatchbyvariable_pa_kernel(tc, x, W, out):
 
         def sel_and_transpose(j):
             g, i = where[j]
-            if i == 0:
-                bucket(g)
             nc.vector.tensor_scalar(
                 out=sel[j][:], in0=colv[:], scalar1=lo[g][:, i : i + 1],
                 scalar2=None, op0=ALU.is_equal,
@@ -189,13 +190,13 @@ def tile_dispatchbyvariable_pa_kernel(tc, x, W, out):
         def first_half(j):
             g, i = where[j]
             nc.scalar.activation(
-                out=part[j][:], in_=acc[(j, 0)][:], func=ACT.Copy, scale=hi0[g][:, i : i + 1]
+                out=part[j][:], in_=acc[(j, 0)][:], func=ACT.Copy, scale=cmp[g][:, i, nb - 1 : nb]
             )
 
         def second_half(j):
             g, i = where[j]
             nc.vector.scalar_tensor_tensor(
-                out=res[j][:], in0=acc[(j, 1)][:], scalar=gt[g][:, i, MID : MID + 1],
+                out=res[j][:], in0=acc[(j, 1)][:], scalar=hi1[g][:, i : i + 1],
                 in1=part[j][:], op0=ALU.mult, op1=ALU.add,
             )
             nc.sync.dma_start(out=o_v[:, j, :], in_=res[j][:])
@@ -216,21 +217,30 @@ def tile_dispatchbyvariable_pa_kernel(tc, x, W, out):
                     stop=(c == L - 1),
                 )
             nc.vector.scalar_tensor_tensor(
-                out=res[j][:, cols], in0=ps[:], scalar=gt[g][:, i, MID : MID + 1],
+                out=res[j][:, cols], in0=ps[:], scalar=hi1[g][:, i : i + 1],
                 in1=part[j][:, cols], op0=ALU.mult, op1=ALU.add,
             )
             nc.sync.dma_start(out=o_v[:, j, cols], in_=res[j][:, cols])
 
+        bucket_cmp(0)
+        bucket_sum(0)
         sel_and_transpose(0)
         sel_and_transpose(1)
         regroup(0)
+        bucket_cmp(1)
+        copy_out(0)
+        quant_w(0)
+        bucket_sum(1)
+        bucket_cmp(2)
         sel_and_transpose(2)
+        bucket_sum(2)
         sel_and_transpose(3)
-        pending = [0]
+        pending = []
         ready_x = []
-        ready_w = []
+        ready_w = [0]
         for j in range(NT):
-            copy_out(j)
+            if j > 0:
+                copy_out(j)
             if 2 <= j < NT - 2:
                 sel_and_transpose(j + 2)
             for k in pending:
@@ -250,8 +260,6 @@ def tile_dispatchbyvariable_pa_kernel(tc, x, W, out):
                     mx(j, k)
         regroup(4)
         regroup(5)
-        for g in range(len(X_GROUPS)):
-            make_hi0(g)
         for j in range(4):
             first_half(j)
         quant_w(4)
@@ -266,6 +274,8 @@ def tile_dispatchbyvariable_pa_kernel(tc, x, W, out):
                 quant_w(6)
             if j == 5:
                 quant_w(7)
+        for g in range(len(X_GROUPS)):
+            make_hi1(g)
         for k in (4, 5):
             for j in range(4):
                 mx(j, k)

@@ -21,10 +21,10 @@ NE = 8
 L = 4
 BOUNDS = (-1.5, -1.0, -0.5, 0.0, 0.5, 1.0, 1.5)
 MID = 3
-FV = [320,320,320,320,320,320,320,320]
+FV = [352,352,352,352,352,352,352,352]
 X_GROUPS = ((0, 1), (2, 3), (4, 5, 6, 7))
 T_BANKS = ((0, 1), (2, 3), (4, 5), (6, 7), (4, 5), (6, 7), (4, 5), (6, 7))
-W_AFTER = {1: (1,), 3: (2,), 5: (3,)}
+W_AFTER = {2: (1,), 4: (2,), 5: (3,)}
 PINNED = True
 
 
@@ -222,6 +222,19 @@ def tile_dispatchbyvariable_pa_kernel(tc, x, W, out):
             )
             nc.sync.dma_start(out=o_v[:, j, cols], in_=res[j][:, cols])
 
+        quantised_x = []
+        quantised_w = []
+        bank_free = [0, 1, 2, 3]
+        issued = []
+
+        def sweep():
+            for j in quantised_x:
+                if j in bank_free:
+                    for k in quantised_w:
+                        if (j, k) not in issued:
+                            issued.append((j, k))
+                            mx(j, k)
+
         bucket_cmp(0)
         bucket_sum(0)
         sel_and_transpose(0)
@@ -230,34 +243,32 @@ def tile_dispatchbyvariable_pa_kernel(tc, x, W, out):
         bucket_cmp(1)
         copy_out(0)
         quant_w(0)
+        quantised_w.append(0)
         bucket_sum(1)
         bucket_cmp(2)
         sel_and_transpose(2)
         bucket_sum(2)
         sel_and_transpose(3)
         pending = []
-        ready_x = []
-        ready_w = [0]
         for j in range(NT):
             if j > 0:
                 copy_out(j)
             if 2 <= j < NT - 2:
                 sel_and_transpose(j + 2)
+            if j >= NT - 2:
+                bank_free.extend(T_BANKS[j])
+                sweep()
             for k in pending:
                 quant_w(k)
-                ready_w.append(k)
-                for t in ready_x:
-                    if t < 4:
-                        mx(t, k)
+                quantised_w.append(k)
+                sweep()
             pending = []
             for k in W_AFTER.get(j, ()):
                 regroup(k)
                 pending.append(k)
             quant_x(j)
-            ready_x.append(j)
-            if j < 4:
-                for k in ready_w:
-                    mx(j, k)
+            quantised_x.append(j)
+            sweep()
         regroup(4)
         regroup(5)
         for j in range(4):
@@ -266,14 +277,12 @@ def tile_dispatchbyvariable_pa_kernel(tc, x, W, out):
         quant_w(5)
         regroup(6)
         regroup(7)
-        for j in range(4, NT):
-            for k in range(L):
-                mx(j, k)
-            first_half(j)
-            if j == 4:
-                quant_w(6)
-            if j == 5:
-                quant_w(7)
+        first_half(4)
+        quant_w(6)
+        first_half(5)
+        quant_w(7)
+        first_half(6)
+        first_half(7)
         for g in range(len(X_GROUPS)):
             make_hi1(g)
         for k in (4, 5):

@@ -25,7 +25,7 @@ FV = [352,352,352,352,352,352,352,352]
 X_GROUPS = ((0, 1), (2, 3), (4, 5, 6, 7))
 T_BANKS = ((0, 1), (2, 3), (4, 5), (6, 7), (4, 5), (6, 7), (4, 5), (6, 7))
 W_AFTER = {2: (1,), 4: (2,), 5: (3,)}
-PINNED = True
+PINNED = False
 
 
 def tile_dispatchbyvariable_pa_kernel(tc, x, W, out):

from contextlib import ExitStack

import concourse.mybir as mybir

FLOPS = 2 * 1024 * 512 * 512 * 8

F32 = mybir.dt.float32
BF16 = mybir.dt.bfloat16
U32 = mybir.dt.uint32
U8 = mybir.dt.uint8
FP8X4 = mybir.dt.float8_e4m3fn_x4
ALU = mybir.AluOpType
ACT = mybir.ActivationFunctionType
AX = mybir.AxisListType

P = 128
NT = 8
D = 512
F = 512
NE = 8
L = 4
BOUNDS = (-1.5, -1.0, -0.5, 0.0, 0.5, 1.0, 1.5)
MID = 3
FV = [352,352,352,352,352,352,352,352]
X_GROUPS = ((0, 1), (2, 3), (4, 5, 6, 7))
T_BANKS = ((0, 1), (2, 3), (4, 5), (6, 7), (4, 5), (6, 7), (4, 5), (6, 7))
W_AFTER = {2: (1,), 4: (2,), 5: (3,)}
PINNED = False


def tile_dispatchbyvariable_pa_kernel(tc, x, W, out):
    nc = tc.nc
    x_v = x.flatten_outer_dims().rearrange("(p j) d -> p j d", j=NT)
    o_v = out.flatten_outer_dims().rearrange("(p j) f -> p j f", j=NT)
    nb = len(BOUNDS)
    where = {}
    for g, tiles in enumerate(X_GROUPS):
        for i, j in enumerate(tiles):
            where[j] = (g, i)

    with ExitStack() as ctx:
        if PINNED:
            ctx.enter_context(tc.manual_schedule())
        keep = ctx.enter_context(tc.tile_pool(name="keep", bufs=1))
        psum = ctx.enter_context(tc.psum_pool(name="psum", bufs=1))

        xh = [keep.tile([P, len(t), D], BF16, name="xh%d" % g) for g, t in enumerate(X_GROUPS)]
        raw = [keep.tile([P, 4, F], BF16, name="raw%d" % k) for k in range(NE)]

        def load_x(g):
            t = X_GROUPS[g]
            nc.sync.dma_start(out=xh[g][:], in_=x_v[:, t[0] : t[0] + len(t), :])

        def load_w(k):
            nc.sync.dma_start(
                out=raw[k][:].rearrange("p (u e) f -> p u (e f)", u=2),
                in_=W[k].rearrange("(u p e) f -> p u (e f)", u=2, e=2),
            )

        load_x(0)
        load_w(0)
        load_x(1)
        load_x(2)
        for k in range(1, NE):
            load_w(k)

        col_i = keep.tile([P, L * P], F32, name="col_i")
        nc.gpsimd.iota(
            col_i[:], pattern=[[1, L * P]], base=0, channel_multiplier=-1,
            allow_small_or_imprecise_dtypes=True,
        )
        bins = keep.tile([P, nb - 1], F32, name="bins")
        for i, b in enumerate(BOUNDS[:MID] + BOUNDS[MID + 1 :]):
            nc.vector.memset(bins[:, i : i + 1], b)
        warm = keep.tile([P, 1], F32, name="warm")
        nc.scalar.activation(out=warm[:], in_=bins[:, 0:1], func=ACT.Copy)
        colv = keep.tile([P, L * P], F32, name="colv")
        nc.vector.tensor_scalar(
            out=colv[:], in0=col_i[:], scalar1=1.0 / P, scalar2=float(MID), op0=ALU.mult, op1=ALU.add
        )

        ncmp = nb - 1 + MID
        cmp = [keep.tile([P, len(t), ncmp], F32, name="cmp%d" % g) for g, t in enumerate(X_GROUPS)]
        lo = [keep.tile([P, len(t)], F32, name="lo%d" % g) for g, t in enumerate(X_GROUPS)]
        hi1 = [keep.tile([P, len(t)], F32, name="hi1_%d" % g) for g, t in enumerate(X_GROUPS)]

        def bucket_cmp(g):
            n = len(X_GROUPS[g])
            nc.vector.tensor_tensor(
                out=cmp[g][:, :, 0 : nb - 1],
                in0=xh[g][:, :, 0:1].to_broadcast([P, n, nb - 1]),
                in1=bins[:].unsqueeze(1).to_broadcast([P, n, nb - 1]),
                op=ALU.is_gt,
            )
            nc.vector.tensor_scalar(
                out=cmp[g][:, :, nb - 1 : ncmp],
                in0=xh[g][:, :, 0:1].to_broadcast([P, n, MID]),
                scalar1=BOUNDS[MID], scalar2=0.0, op0=ALU.is_gt, op1=ALU.is_equal,
            )

        def bucket_sum(g):
            nc.vector.tensor_reduce(out=lo[g][:], in_=cmp[g][:], axis=AX.X, op=ALU.add)

        def make_hi1(g):
            nc.vector.tensor_scalar(
                out=hi1[g][:], in0=xh[g][:, :, 0], scalar1=BOUNDS[MID], scalar2=None, op0=ALU.is_gt
            )

        sel = [keep.tile([P, L * P], F32, name="sel%d" % j) for j in range(NT)]
        xg = [keep.tile([P, L * P * 4], BF16, name="xg%d" % j, align_bytes=64) for j in range(NT)]
        xq = [keep.tile([P, L * P], U32, name="xq%d" % j, align_bytes=64) for j in range(NT)]
        xs = [keep.tile([P, L * P], U8, name="xs%d" % j, align_bytes=64) for j in range(NT)]
        pts = {}

        def sel_and_transpose(j):
            g, i = where[j]
            nc.vector.tensor_scalar(
                out=sel[j][:], in0=colv[:], scalar1=lo[g][:, i : i + 1],
                scalar2=None, op0=ALU.is_equal,
            )
            words = xh[g][:].rearrange("p j d -> p (j d)").bitcast(F32)
            for half in range(2):
                pt = psum.tile(
                    [P, 2, 2, P], F32, tag="bank%d" % T_BANKS[j][half], name="pt%d_%d" % (j, half)
                )
                pts[(j, half)] = pt
                for u in range(2):
                    c0 = i * (D // 2) + u * P
                    for li in range(2):
                        c = 2 * half + li
                        nc.tensor.transpose(
                            out=pt[:, li, u, :],
                            in_=words[:, c0 : c0 + P],
                            identity=sel[j][:, c * P : (c + 1) * P],
                        )

        def copy_out(j):
            dst = xg[j][:].bitcast(F32).rearrange("p (l t u) -> p l t u", l=L, u=2)
            for half in range(2):
                nc.scalar.copy(
                    out=dst[:, 2 * half : 2 * half + 2, :, :],
                    in_=pts[(j, half)][:].rearrange("p l u t -> p l t u"),
                )

        def quant_x(j):
            nc.vector.quantize_mx(out=xq[j][:].bitcast(FP8X4), scales=xs[j][:], in_=xg[j][:])

        wg = [keep.tile([P, F, 4], BF16, name="wg%d" % k, align_bytes=64) for k in range(NE)]
        wq = [keep.tile([P, F], U32, name="wq%d" % k, align_bytes=64) for k in range(NE)]
        ws = [keep.tile([P, F], U8, name="ws%d" % k, align_bytes=64) for k in range(NE)]

        def regroup(k):
            fv = FV[k]
            if fv > 0:
                nc.vector.tensor_copy(
                    out=wg[k][:, 0:fv, :].rearrange("p (c i) t -> p c t i", i=4),
                    in_=raw[k][:, :, 0:fv].rearrange("p t (c i) -> p c t i", i=4),
                )
            if fv < F:
                nc.scalar.copy(
                    out=wg[k][:, fv:F, :].rearrange("p (c i) t -> p c t i", i=4),
                    in_=raw[k][:, :, fv:F].rearrange("p t (c i) -> p c t i", i=4),
                )

        def quant_w(k):
            nc.vector.quantize_mx(
                out=wq[k][:].bitcast(FP8X4), scales=ws[k][:],
                in_=wg[k][:].rearrange("p f t -> p (f t)"),
            )

        acc = {}

        def mx(j, k):
            h, c = k // L, k % L
            if c == 0:
                acc[(j, h)] = psum.tile([P, F], F32, tag="bank%d" % j, name="acc%d_%d" % (j, h))
            nc.tensor.matmul_mx(
                out=acc[(j, h)][:],
                lhsT=xq[j][:, c * P : (c + 1) * P].bitcast(FP8X4),
                lhsT_scale=xs[j][:, c * P : (c + 1) * P],
                rhs=wq[k][:].bitcast(FP8X4),
                rhs_scale=ws[k][:],
                start=(c == 0),
                stop=(c == L - 1),
            )

        part = [keep.tile([P, F], F32, name="part%d" % j) for j in range(NT)]
        res = [keep.tile([P, F], F32, name="res%d" % j) for j in range(NT)]

        def first_half(j):
            g, i = where[j]
            nc.scalar.activation(
                out=part[j][:], in_=acc[(j, 0)][:], func=ACT.Copy, scale=cmp[g][:, i, nb - 1 : nb]
            )

        def second_half(j):
            g, i = where[j]
            nc.vector.scalar_tensor_tensor(
                out=res[j][:], in0=acc[(j, 1)][:], scalar=hi1[g][:, i : i + 1],
                in1=part[j][:], op0=ALU.mult, op1=ALU.add,
            )
            nc.sync.dma_start(out=o_v[:, j, :], in_=res[j][:])

        def last_tile_half(half, bank):
            j = NT - 1
            g, i = where[j]
            cols = slice(half * (F // 2), (half + 1) * (F // 2))
            ps = psum.tile([P, F // 2], F32, tag="bank%d" % bank, name="last%d" % half)
            for c in range(L):
                nc.tensor.matmul_mx(
                    out=ps[:],
                    lhsT=xq[j][:, c * P : (c + 1) * P].bitcast(FP8X4),
                    lhsT_scale=xs[j][:, c * P : (c + 1) * P],
                    rhs=wq[L + c][:, cols].bitcast(FP8X4),
                    rhs_scale=ws[L + c][:, cols],
                    start=(c == 0),
                    stop=(c == L - 1),
                )
            nc.vector.scalar_tensor_tensor(
                out=res[j][:, cols], in0=ps[:], scalar=hi1[g][:, i : i + 1],
                in1=part[j][:, cols], op0=ALU.mult, op1=ALU.add,
            )
            nc.sync.dma_start(out=o_v[:, j, cols], in_=res[j][:, cols])

        quantised_x = []
        quantised_w = []
        bank_free = [0, 1, 2, 3]
        issued = []

        def sweep():
            for j in quantised_x:
                if j in bank_free:
                    for k in quantised_w:
                        if (j, k) not in issued:
                            issued.append((j, k))
                            mx(j, k)

        bucket_cmp(0)
        bucket_sum(0)
        sel_and_transpose(0)
        sel_and_transpose(1)
        regroup(0)
        bucket_cmp(1)
        copy_out(0)
        quant_w(0)
        quantised_w.append(0)
        bucket_sum(1)
        bucket_cmp(2)
        sel_and_transpose(2)
        bucket_sum(2)
        sel_and_transpose(3)
        pending = []
        for j in range(NT):
            if j > 0:
                copy_out(j)
            if 2 <= j < NT - 2:
                sel_and_transpose(j + 2)
            if j >= NT - 2:
                bank_free.extend(T_BANKS[j])
                sweep()
            for k in pending:
                quant_w(k)
                quantised_w.append(k)
                sweep()
            pending = []
            for k in W_AFTER.get(j, ()):
                regroup(k)
                pending.append(k)
            quant_x(j)
            quantised_x.append(j)
            sweep()
        regroup(4)
        regroup(5)
        for j in range(4):
            first_half(j)
        quant_w(4)
        quant_w(5)
        regroup(6)
        regroup(7)
        first_half(4)
        quant_w(6)
        first_half(5)
        quant_w(7)
        first_half(6)
        first_half(7)
        for g in range(len(X_GROUPS)):
            make_hi1(g)
        for k in (4, 5):
            for j in range(4):
                mx(j, k)
        for j in range(4):
            mx(j, 6)
            mx(j, 7)
            second_half(j)
        for j in range(4, NT - 1):
            for k in range(L, NE):
                mx(j, k)
            second_half(j)
        for half, bank in enumerate((NT - 1, 0)):
            last_tile_half(half, bank)
